import numpy as np
import ml_dtypes


def mxq(x, axis, fmt="e4m3"):
    dtype, down = {"e4m3": (ml_dtypes.float8_e4m3fn, 7), "e5m2": (ml_dtypes.float8_e5m2, 14)}[fmt]
    v = np.moveaxis(np.asarray(x, np.float32).astype(ml_dtypes.bfloat16).astype(np.float64), axis, -1)
    blocks = v.reshape(v.shape[:-1] + (-1, 32))
    amax = np.abs(blocks).max(-1, keepdims=True)
    byte = np.maximum(np.where(amax > 0, np.frexp(amax)[1] - 1 + 127, 0) - down, 1)
    scale = np.exp2(byte - 127.0)
    codes = (blocks / scale).astype(np.float32).astype(dtype).astype(np.float64)
    return np.moveaxis((codes * scale).reshape(v.shape), -1, axis)


WIDE = False


def mx_kscale(k):
    if not WIDE:
        return np.ones(k)
    levels = np.array([10, -10, 5, -5, 0])
    a = np.random.permutation(np.resize(levels, k // 512 * 4)).reshape(k // 512, 4)
    idx = np.arange(k)
    return np.exp2(a[idx // 512, idx % 128 // 32])


BF16 = ml_dtypes.bfloat16


def bf(x):
    return np.asarray(x, np.float32).astype(BF16)


def f64(x):
    return np.asarray(x).astype(np.float64)


B, S, D, H, DK, F = 2, 256, 1024, 8, 128, 2560
HD = H * DK
EPS = 1e-6


def rmsnorm(v, g):
    return v / np.sqrt(np.mean(v * v, axis=-1, keepdims=True) + EPS) * g


def silu(v):
    return v / (1.0 + np.exp(-v))


def setup_inputs():
    s, t = mx_kscale(HD), mx_kscale(D)
    return {"x": bf(np.random.standard_normal((B, S, D))),
            "ao": bf(np.random.standard_normal((B, H, S, DK)) * 0.3 * s.reshape(H, 1, DK)),
            "wo": bf(np.random.standard_normal((HD, D)) * 1.5 / np.sqrt(HD) / s[:, None]),
            "bo": bf(np.random.standard_normal(D) * 0.1),
            "g2": bf((1.0 + 0.1 * np.random.standard_normal(D)) * t),
            "w1": bf(np.random.standard_normal((D, F)) / np.sqrt(D) / t[:, None]),
            "w3": bf(np.random.standard_normal((D, F)) / np.sqrt(D) / t[:, None])}


def reference(x, ao, wo, bo, g2, w1, w3):
    a = f64(ao).transpose(0, 2, 1, 3).reshape(B, S, HD)
    x1 = f64(x) + ((mxq(a, 2, "e4m3") @ mxq(f64(wo), 0, "e4m3")) + f64(bo))
    n = mxq(rmsnorm(x1, f64(g2)), 2, "e4m3")
    h = silu(n @ mxq(f64(w1), 0, "e4m3")) * (n @ mxq(f64(w3), 0, "e4m3"))
    return x1, h

@@ -1,0 +1,195 @@
+from contextlib import ExitStack
+
+import concourse.mybir as mybir
+from concourse.masks import make_identity
+
+F32 = mybir.dt.float32
+BF16 = mybir.dt.bfloat16
+U32 = mybir.dt.uint32
+U8 = mybir.dt.uint8
+FP8X4 = mybir.dt.float8_e4m3fn_x4
+ACT = mybir.ActivationFunctionType
+ALU = mybir.AluOpType
+
+B, S, D, H, DK, F = 2, 256, 1024, 8, 128, 2560
+EPS = 1e-6
+
+P = 128
+PACK = 4
+K_PASS = P * PACK
+PASSES = D // K_PASS
+N_TILE = 512
+SLAB_COLS = 1024
+RAW_BUFS = 4
+SCALAR_COLS = 256
+
+FLOPS = 2 * B * S * D * (D + 2 * F)
+
+
+def tile_transformerblock_pb_kernel(tc, x, ao, wo, bo, g2, w1, w3, out_0, out_1):
+    nc = tc.nc
+
+    token_tiles = [(b, i) for b in range(B) for i in range(2)]
+    ao_rows = ao.rearrange("b h (p i) d -> b p h (i d)", i=2)
+    x_rows = x.rearrange("b (p i) d -> b p (i d)", i=2)
+    x1_rows = out_0.rearrange("b (p i) d -> b i p d", i=2)
+    h_rows = out_1.rearrange("b (p i) f -> b i p f", i=2)
+
+    slabs = [(wo, 0, D)]
+    for c0 in range(0, F, SLAB_COLS):
+        for w in (w1, w3):
+            slabs.append((w, c0, min(SLAB_COLS, F - c0)))
+
+    with ExitStack() as ctx:
+        const = ctx.enter_context(tc.tile_pool(name="const", bufs=1))
+        acts = ctx.enter_context(tc.tile_pool(name="acts", bufs=1))
+        raw_pool = ctx.enter_context(tc.tile_pool(name="raw", bufs=RAW_BUFS))
+        grouped_pool = ctx.enter_context(tc.tile_pool(name="grouped", bufs=4))
+        mx_pool = ctx.enter_context(tc.tile_pool(name="mx", bufs=1))
+        work = ctx.enter_context(tc.tile_pool(name="work", bufs=2))
+        out_pool = ctx.enter_context(tc.tile_pool(name="out", bufs=3))
+        psum = ctx.enter_context(tc.psum_pool(name="psum", bufs=8))
+
+        raw_slabs = {}
+        slab_codes = {}
+        slab_scales = {}
+
+        def load_slab(s):
+            w, c0, width = slabs[s]
+            rows = w.rearrange("(g t p) n -> g p t n", g=PASSES, t=PACK)
+            raw = raw_pool.tile([P, PASSES, PACK, SLAB_COLS], BF16, tag="raw")
+            for g in range(PASSES):
+                nc.sync.dma_start(out=raw[:, g, :, :width], in_=rows[g][:, :, c0 : c0 + width])
+            raw_slabs[s] = raw
+
+        def quantise_slab(s):
+            width = slabs[s][2]
+            raw = raw_slabs[s]
+            codes = mx_pool.tile([P, PASSES, width], U32, name="codes%d" % s, align_bytes=64)
+            scales = mx_pool.tile([P, PASSES, width], U8, name="scales%d" % s, align_bytes=64)
+            for g in range(PASSES):
+                for c in range(0, width, N_TILE):
+                    grouped = grouped_pool.tile([P, N_TILE, PACK], BF16, align_bytes=64)
+                    for copy, lo, hi in (
+                        (nc.scalar.copy, 0, SCALAR_COLS),
+                        (nc.vector.tensor_copy, SCALAR_COLS, N_TILE),
+                    ):
+                        copy(
+                            out=grouped[:, lo:hi, :].rearrange("p (c i) t -> p c t i", i=4),
+                            in_=raw[:, g, :, c + lo : c + hi].rearrange("p t (c i) -> p c t i", i=4),
+                        )
+                    nc.vector.quantize_mx(
+                        out=codes[:, g, c : c + N_TILE].bitcast(FP8X4),
+                        scales=scales[:, g, c : c + N_TILE],
+                        in_=grouped[:].rearrange("p w t -> p (w t)"),
+                    )
+            slab_codes[s] = codes
+            slab_scales[s] = scales
+
+        def quantise_transposed(rows_of, codes, scales):
+            flipped = psum.tile([P, PASSES * PACK, P], BF16, tag="bank")
+            for c in range(PASSES * PACK):
+                nc.tensor.transpose(out=flipped[:, c, :], in_=rows_of(c), identity=ident[:])
+            grouped_act = work.tile([P, PASSES, P, PACK], BF16, align_bytes=64)
+            nc.scalar.copy(out=grouped_act[:], in_=flipped[:].rearrange("p (g t) r -> p g r t", t=PACK))
+            nc.vector.quantize_mx(
+                out=codes.rearrange("p g r -> p (g r)").bitcast(FP8X4),
+                scales=scales.rearrange("p g r -> p (g r)"),
+                in_=grouped_act[:].rearrange("p g r t -> p (g r t)"),
+            )
+
+        def contract(acc, m, act_codes, act_scales, s, c):
+            for g in range(PASSES):
+                nc.tensor.matmul_mx(
+                    out=acc[:],
+                    lhsT=act_codes[:, m, g, :].bitcast(FP8X4),
+                    lhsT_scale=act_scales[:, m, g, :],
+                    rhs=slab_codes[s][:, g, c : c + N_TILE].bitcast(FP8X4),
+                    rhs_scale=slab_scales[s][:, g, c : c + N_TILE],
+                    start=(g == 0),
+                    stop=(g == PASSES - 1),
+                )
+
+        ident = const.tile([P, P], BF16)
+        make_identity(nc, ident[:])
+        eps = const.tile([P, 1], F32)
+        nc.vector.memset(eps[:], EPS)
+        warm = const.tile([P, 1], F32)
+        nc.scalar.activation(out=warm[:], in_=eps[:], func=ACT.Sqrt)
+
+        a_sb = acts.tile([P, B, H, 2, DK], BF16)
+        x_sb = acts.tile([P, B, 2, D], BF16)
+        for b in range(B):
+            nc.sync.dma_start(out=a_sb[:, b].rearrange("p h i d -> p h (i d)"), in_=ao_rows[b])
+        load_slab(0)
+        for b in range(B):
+            nc.sync.dma_start(out=x_sb[:, b].rearrange("p i d -> p (i d)"), in_=x_rows[b])
+        bo_all = const.tile([P, D], BF16)
+        g2_all = const.tile([P, D], BF16)
+        nc.scalar.dma_start(out=bo_all[:], in_=bo.partition_broadcast(P))
+        nc.scalar.dma_start(out=g2_all[:], in_=g2.partition_broadcast(P))
+        for s in range(1, RAW_BUFS):
+            load_slab(s)
+
+        a_codes = acts.tile([P, len(token_tiles), PASSES, P], U32, align_bytes=64)
+        a_scales = acts.tile([P, len(token_tiles), PASSES, P], U8, align_bytes=64)
+        for m, (b, i) in enumerate(token_tiles):
+            quantise_transposed(lambda h: a_sb[:, b, h, i, :], a_codes[:, m], a_scales[:, m])
+        quantise_slab(0)
+        load_slab(RAW_BUFS)
+
+        x1 = []
+        sum_sq = const.tile([P, len(token_tiles)], F32)
+        for m, (b, i) in enumerate(token_tiles):
+            x1_m = acts.tile([P, D], F32, name="x1_%d" % m)
+            x1.append(x1_m)
+            nc.vector.tensor_tensor(out=x1_m[:], in0=x_sb[:, b, i, :], in1=bo_all[:], op=ALU.add)
+        for m, (b, i) in enumerate(token_tiles):
+            for c in range(0, D, N_TILE):
+                acc = psum.tile([P, N_TILE], F32, tag="bank")
+                contract(acc, m, a_codes, a_scales, 0, c)
+                nc.vector.tensor_tensor(
+                    out=x1[m][:, c : c + N_TILE], in0=acc[:], in1=x1[m][:, c : c + N_TILE], op=ALU.add
+                )
+            nc.gpsimd.dma_start(out=x1_rows[b, i], in_=x1[m][:])
+            squares = work.tile([P, D], BF16)
+            nc.scalar.activation(
+                out=squares[:], in_=x1[m][:], func=ACT.Square, accum_out=sum_sq[:, m : m + 1]
+            )
+
+        rms = const.tile([P, len(token_tiles)], F32)
+        nc.scalar.activation(out=rms[:], in_=sum_sq[:], func=ACT.Sqrt, scale=1.0 / D, bias=eps[:])
+        inv_rms = const.tile([P, len(token_tiles)], F32)
+        nc.vector.reciprocal(out=inv_rms[:], in_=rms[:])
+        n_codes = acts.tile([P, len(token_tiles), PASSES, P], U32, align_bytes=64)
+        n_scales = acts.tile([P, len(token_tiles), PASSES, P], U8, align_bytes=64)
+        for m in range(len(token_tiles)):
+            n_sb = work.tile([P, D], BF16)
+            nc.vector.scalar_tensor_tensor(
+                out=n_sb[:],
+                in0=x1[m][:],
+                scalar=inv_rms[:, m : m + 1],
+                in1=g2_all[:],
+                op0=ALU.mult,
+                op1=ALU.mult,
+            )
+            quantise_transposed(lambda c: n_sb[:, c * P : (c + 1) * P], n_codes[:, m], n_scales[:, m])
+
+        for s1 in range(1, len(slabs), 2):
+            s3 = s1 + 1
+            c0, width = slabs[s1][1], slabs[s1][2]
+            for s in (s1, s3):
+                quantise_slab(s)
+                if s + RAW_BUFS < len(slabs):
+                    load_slab(s + RAW_BUFS)
+            for m, (b, i) in enumerate(token_tiles):
+                h_sb = out_pool.tile([P, SLAB_COLS], F32)
+                for c in range(0, width, N_TILE):
+                    u = psum.tile([P, N_TILE], F32, tag="bank")
+                    v = psum.tile([P, N_TILE], F32, tag="bank")
+                    contract(u, m, n_codes, n_scales, s1, c)
+                    contract(v, m, n_codes, n_scales, s3, c)
+                    gate = out_pool.tile([P, N_TILE], F32)
+                    nc.scalar.activation(out=gate[:], in_=u[:], func=ACT.Silu)
+                    nc.vector.tensor_tensor(out=h_sb[:, c : c + N_TILE], in0=v[:], in1=gate[:], op=ALU.mult)
+                nc.gpsimd.dma_start(out=h_rows[b, i][:, c0 : c0 + width], in_=h_sb[:, :width])

@@ -39,6 +39,10 @@ def tile_transformerblock_pb_kernel(tc, x, ao, wo, bo, g2, w1, w3, out_0, out_1)
     for c0 in range(0, F, SLAB_COLS):
         for w in (w1, w3):
             slabs.append((w, c0, min(SLAB_COLS, F - c0)))
+    pieces = [
+        (s, g, c) for s in range(len(slabs)) for g in range(PASSES) for c in range(0, slabs[s][2], N_TILE)
+    ]
+    wo_pieces = PASSES * D // N_TILE
 
     with ExitStack() as ctx:
         const = ctx.enter_context(tc.tile_pool(name="const", bufs=1))
@@ -49,10 +53,13 @@ def tile_transformerblock_pb_kernel(tc, x, ao, wo, bo, g2, w1, w3, out_0, out_1)
         work = ctx.enter_context(tc.tile_pool(name="work", bufs=2))
         out_pool = ctx.enter_context(tc.tile_pool(name="out", bufs=3))
         psum = ctx.enter_context(tc.psum_pool(name="psum", bufs=8))
+        ctx.enter_context(tc.manual_schedule())
 
         raw_slabs = {}
-        slab_codes = {}
-        slab_scales = {}
+        grouped_pieces = {}
+        piece_codes = {}
+        piece_scales = {}
+        progress = {"steps": 0}
 
         def load_slab(s):
             w, c0, width = slabs[s]
@@ -62,50 +69,67 @@ def tile_transformerblock_pb_kernel(tc, x, ao, wo, bo, g2, w1, w3, out_0, out_1)
                 nc.sync.dma_start(out=raw[:, g, :, :width], in_=rows[g][:, :, c0 : c0 + width])
             raw_slabs[s] = raw
 
-        def quantise_slab(s):
-            width = slabs[s][2]
-            raw = raw_slabs[s]
-            codes = mx_pool.tile([P, PASSES, width], U32, name="codes%d" % s, align_bytes=64)
-            scales = mx_pool.tile([P, PASSES, width], U8, name="scales%d" % s, align_bytes=64)
-            for g in range(PASSES):
-                for c in range(0, width, N_TILE):
-                    grouped = grouped_pool.tile([P, N_TILE, PACK], BF16, align_bytes=64)
-                    for copy, lo, hi in (
-                        (nc.scalar.copy, 0, SCALAR_COLS),
-                        (nc.vector.tensor_copy, SCALAR_COLS, N_TILE),
-                    ):
-                        copy(
-                            out=grouped[:, lo:hi, :].rearrange("p (c i) t -> p c t i", i=4),
-                            in_=raw[:, g, :, c + lo : c + hi].rearrange("p t (c i) -> p c t i", i=4),
-                        )
-                    nc.vector.quantize_mx(
-                        out=codes[:, g, c : c + N_TILE].bitcast(FP8X4),
-                        scales=scales[:, g, c : c + N_TILE],
-                        in_=grouped[:].rearrange("p w t -> p (w t)"),
-                    )
-            slab_codes[s] = codes
-            slab_scales[s] = scales
+        def regroup(k):
+            s, g, c = pieces[k]
+            grouped = grouped_pool.tile([P, N_TILE, PACK], BF16, align_bytes=64)
+            for copy, lo, hi in (
+                (nc.scalar.copy, 0, SCALAR_COLS),
+                (nc.vector.tensor_copy, SCALAR_COLS, N_TILE),
+            ):
+                copy(
+                    out=grouped[:, lo:hi, :].rearrange("p (c i) t -> p c t i", i=4),
+                    in_=raw_slabs[s][:, g, :, c + lo : c + hi].rearrange("p t (c i) -> p c t i", i=4),
+                )
+            grouped_pieces[k] = grouped
+            last_of_slab = k + 1 == len(pieces) or pieces[k + 1][0] != s
+            if last_of_slab and s + RAW_BUFS < len(slabs):
+                load_slab(s + RAW_BUFS)
 
-        def quantise_transposed(rows_of, codes, scales):
+        def quantise(k):
+            codes = mx_pool.tile([P, N_TILE], U32, name="codes%d" % k, align_bytes=64)
+            scales = mx_pool.tile([P, N_TILE], U8, name="scales%d" % k, align_bytes=64)
+            nc.vector.quantize_mx(
+                out=codes[:].bitcast(FP8X4),
+                scales=scales[:],
+                in_=grouped_pieces[k][:].rearrange("p w t -> p (w t)"),
+            )
+            piece_codes[pieces[k]] = codes
+            piece_scales[pieces[k]] = scales
+
+        def weight_step():
+            k = progress["steps"]
+            if k < len(pieces):
+                regroup(k)
+            if 1 <= k <= len(pieces):
+                quantise(k - 1)
+            progress["steps"] = k + 1
+
+        def transpose_blocks(rows_of):
             flipped = psum.tile([P, PASSES * PACK, P], BF16, tag="bank")
             for c in range(PASSES * PACK):
                 nc.tensor.transpose(out=flipped[:, c, :], in_=rows_of(c), identity=ident[:])
+            return flipped
+
+        def group_words(flipped):
             grouped_act = work.tile([P, PASSES, P, PACK], BF16, align_bytes=64)
             nc.scalar.copy(out=grouped_act[:], in_=flipped[:].rearrange("p (g t) r -> p g r t", t=PACK))
+            return grouped_act
+
+        def quantise_tokens(grouped_act, codes, scales):
             nc.vector.quantize_mx(
                 out=codes.rearrange("p g r -> p (g r)").bitcast(FP8X4),
                 scales=scales.rearrange("p g r -> p (g r)"),
                 in_=grouped_act[:].rearrange("p g r t -> p (g r t)"),
             )
 
-        def contract(acc, m, act_codes, act_scales, s, c):
+        def contract(acc, act_codes, act_scales, m, s, c):
             for g in range(PASSES):
                 nc.tensor.matmul_mx(
                     out=acc[:],
                     lhsT=act_codes[:, m, g, :].bitcast(FP8X4),
                     lhsT_scale=act_scales[:, m, g, :],
-                    rhs=slab_codes[s][:, g, c : c + N_TILE].bitcast(FP8X4),
-                    rhs_scale=slab_scales[s][:, g, c : c + N_TILE],
+                    rhs=piece_codes[(s, g, c)][:].bitcast(FP8X4),
+                    rhs_scale=piece_scales[(s, g, c)][:],
                     start=(g == 0),
                     stop=(g == PASSES - 1),
                 )
@@ -114,6 +138,9 @@ def tile_transformerblock_pb_kernel(tc, x, ao, wo, bo, g2, w1, w3, out_0, out_1)
         make_identity(nc, ident[:])
         eps = const.tile([P, 1], F32)
         nc.vector.memset(eps[:], EPS)
+        bo_all = const.tile([P, D], BF16)
+        g2_all = const.tile([P, D], BF16)
+        nc.scalar.dma_start(out=bo_all[:], in_=bo.partition_broadcast(P))
         warm = const.tile([P, 1], F32)
         nc.scalar.activation(out=warm[:], in_=eps[:], func=ACT.Sqrt)
 
@@ -121,37 +148,34 @@ def tile_transformerblock_pb_kernel(tc, x, ao, wo, bo, g2, w1, w3, out_0, out_1)
         x_sb = acts.tile([P, B, 2, D], BF16)
         for b in range(B):
             nc.sync.dma_start(out=a_sb[:, b].rearrange("p h i d -> p h (i d)"), in_=ao_rows[b])
-        load_slab(0)
-        for b in range(B):
             nc.sync.dma_start(out=x_sb[:, b].rearrange("p i d -> p (i d)"), in_=x_rows[b])
-        bo_all = const.tile([P, D], BF16)
-        g2_all = const.tile([P, D], BF16)
-        nc.scalar.dma_start(out=bo_all[:], in_=bo.partition_broadcast(P))
-        nc.scalar.dma_start(out=g2_all[:], in_=g2.partition_broadcast(P))
+        load_slab(0)
+        nc.sync.dma_start(out=g2_all[:], in_=g2.partition_broadcast(P))
         for s in range(1, RAW_BUFS):
             load_slab(s)
 
         a_codes = acts.tile([P, len(token_tiles), PASSES, P], U32, align_bytes=64)
         a_scales = acts.tile([P, len(token_tiles), PASSES, P], U8, align_bytes=64)
-        for m, (b, i) in enumerate(token_tiles):
-            quantise_transposed(lambda h: a_sb[:, b, h, i, :], a_codes[:, m], a_scales[:, m])
-        quantise_slab(0)
-        load_slab(RAW_BUFS)
-
         x1 = []
-        sum_sq = const.tile([P, len(token_tiles)], F32)
         for m, (b, i) in enumerate(token_tiles):
+            grouped_a = group_words(transpose_blocks(lambda h: a_sb[:, b, h, i, :]))
             x1_m = acts.tile([P, D], F32, name="x1_%d" % m)
             x1.append(x1_m)
             nc.vector.tensor_tensor(out=x1_m[:], in0=x_sb[:, b, i, :], in1=bo_all[:], op=ALU.add)
-        for m, (b, i) in enumerate(token_tiles):
+            quantise_tokens(grouped_a, a_codes[:, m], a_scales[:, m])
+
+        for k in range(wo_pieces + 2):
+            weight_step()
+
+        sum_sq = const.tile([P, len(token_tiles)], F32)
+        for m in range(len(token_tiles)):
             for c in range(0, D, N_TILE):
                 acc = psum.tile([P, N_TILE], F32, tag="bank")
-                contract(acc, m, a_codes, a_scales, 0, c)
+                contract(acc, a_codes, a_scales, m, 0, c)
                 nc.vector.tensor_tensor(
                     out=x1[m][:, c : c + N_TILE], in0=acc[:], in1=x1[m][:, c : c + N_TILE], op=ALU.add
                 )
-            nc.gpsimd.dma_start(out=x1_rows[b, i], in_=x1[m][:])
+            weight_step()
             squares = work.tile([P, D], BF16)
             nc.scalar.activation(
                 out=squares[:], in_=x1[m][:], func=ACT.Square, accum_out=sum_sq[:, m : m + 1]
@@ -163,33 +187,40 @@ def tile_transformerblock_pb_kernel(tc, x, ao, wo, bo, g2, w1, w3, out_0, out_1)
         nc.vector.reciprocal(out=inv_rms[:], in_=rms[:])
         n_codes = acts.tile([P, len(token_tiles), PASSES, P], U32, align_bytes=64)
         n_scales = acts.tile([P, len(token_tiles), PASSES, P], U8, align_bytes=64)
-        for m in range(len(token_tiles)):
-            n_sb = work.tile([P, D], BF16)
-            nc.vector.scalar_tensor_tensor(
-                out=n_sb[:],
-                in0=x1[m][:],
-                scalar=inv_rms[:, m : m + 1],
-                in1=g2_all[:],
-                op0=ALU.mult,
-                op1=ALU.mult,
-            )
-            quantise_transposed(lambda c: n_sb[:, c * P : (c + 1) * P], n_codes[:, m], n_scales[:, m])
+        grouped_n = {}
+        for m in range(len(token_tiles) + 1):
+            if m < len(token_tiles):
+                n_sb = work.tile([P, D], BF16)
+                nc.vector.scalar_tensor_tensor(
+                    out=n_sb[:],
+                    in0=x1[m][:],
+                    scalar=inv_rms[:, m : m + 1],
+                    in1=g2_all[:],
+                    op0=ALU.mult,
+                    op1=ALU.mult,
+                )
+                flipped_n = transpose_blocks(lambda c: n_sb[:, c * P : (c + 1) * P])
+            weight_step()
+            if m < len(token_tiles):
+                grouped_n[m] = group_words(flipped_n)
+            if m > 0:
+                quantise_tokens(grouped_n[m - 1], n_codes[:, m - 1], n_scales[:, m - 1])
+
+        for m, (b, i) in enumerate(token_tiles):
+            nc.sync.dma_start(out=x1_rows[b, i], in_=x1[m][:])
 
         for s1 in range(1, len(slabs), 2):
             s3 = s1 + 1
             c0, width = slabs[s1][1], slabs[s1][2]
-            for s in (s1, s3):
-                quantise_slab(s)
-                if s + RAW_BUFS < len(slabs):
-                    load_slab(s + RAW_BUFS)
             for m, (b, i) in enumerate(token_tiles):
                 h_sb = out_pool.tile([P, SLAB_COLS], F32)
                 for c in range(0, width, N_TILE):
                     u = psum.tile([P, N_TILE], F32, tag="bank")
                     v = psum.tile([P, N_TILE], F32, tag="bank")
-                    contract(u, m, n_codes, n_scales, s1, c)
-                    contract(v, m, n_codes, n_scales, s3, c)
+                    contract(u, n_codes, n_scales, m, s1, c)
+                    contract(v, n_codes, n_scales, m, s3, c)
                     gate = out_pool.tile([P, N_TILE], F32)
                     nc.scalar.activation(out=gate[:], in_=u[:], func=ACT.Silu)
+                    weight_step()
                     nc.vector.tensor_tensor(out=h_sb[:, c : c + N_TILE], in0=v[:], in1=gate[:], op=ALU.mult)
-                nc.gpsimd.dma_start(out=h_rows[b, i][:, c0 : c0 + width], in_=h_sb[:, :width])
+                nc.sync.dma_start(out=h_rows[b, i][:, c0 : c0 + width], in_=h_sb[:, :width])

@@ -7,6 +7,7 @@ F32 = mybir.dt.float32
 BF16 = mybir.dt.bfloat16
 U32 = mybir.dt.uint32
 U8 = mybir.dt.uint8
+I32 = mybir.dt.int32
 FP8X4 = mybir.dt.float8_e4m3fn_x4
 ACT = mybir.ActivationFunctionType
 ALU = mybir.AluOpType
@@ -35,14 +36,16 @@ def tile_transformerblock_pb_kernel(tc, x, ao, wo, bo, g2, w1, w3, out_0, out_1)
     x1_rows = out_0.rearrange("b (p i) d -> b i p d", i=2)
     h_rows = out_1.rearrange("b (p i) f -> b i p f", i=2)
 
-    slabs = [(wo, 0, D)]
+    groups = [[(wo, 0, D)]]
     for c0 in range(0, F, SLAB_COLS):
-        for w in (w1, w3):
-            slabs.append((w, c0, min(SLAB_COLS, F - c0)))
+        groups.append([(w, c0, min(SLAB_COLS, F - c0)) for w in (w1, w3)])
     pieces = [
-        (s, g, c) for s in range(len(slabs)) for g in range(PASSES) for c in range(0, slabs[s][2], N_TILE)
+        (q, g, c, j)
+        for q in range(len(groups))
+        for g in range(PASSES)
+        for c in range(0, groups[q][0][2], N_TILE)
+        for j in range(len(groups[q]))
     ]
-    wo_pieces = PASSES * D // N_TILE
 
     with ExitStack() as ctx:
         const = ctx.enter_context(tc.tile_pool(name="const", bufs=1))
@@ -51,7 +54,7 @@ def tile_transformerblock_pb_kernel(tc, x, ao, wo, bo, g2, w1, w3, out_0, out_1)
         grouped_pool = ctx.enter_context(tc.tile_pool(name="grouped", bufs=4))
         mx_pool = ctx.enter_context(tc.tile_pool(name="mx", bufs=1))
         work = ctx.enter_context(tc.tile_pool(name="work", bufs=2))
-        out_pool = ctx.enter_context(tc.tile_pool(name="out", bufs=3))
+        out_pool = ctx.enter_context(tc.tile_pool(name="out", bufs=4))
         psum = ctx.enter_context(tc.psum_pool(name="psum", bufs=8))
         ctx.enter_context(tc.manual_schedule())
 
@@ -61,16 +64,20 @@ def tile_transformerblock_pb_kernel(tc, x, ao, wo, bo, g2, w1, w3, out_0, out_1)
         piece_scales = {}
         progress = {"steps": 0}
 
-        def load_slab(s):
-            w, c0, width = slabs[s]
-            rows = w.rearrange("(g t p) n -> g p t n", g=PASSES, t=PACK)
-            raw = raw_pool.tile([P, PASSES, PACK, SLAB_COLS], BF16, tag="raw")
+        def load_group(q):
+            for j in range(len(groups[q])):
+                raw_slabs[(q, j)] = raw_pool.tile(
+                    [P, PASSES, PACK, SLAB_COLS], BF16, tag="raw", name="raw%d_%d" % (q, j)
+                )
             for g in range(PASSES):
-                nc.sync.dma_start(out=raw[:, g, :, :width], in_=rows[g][:, :, c0 : c0 + width])
-            raw_slabs[s] = raw
+                for j, (w, c0, width) in enumerate(groups[q]):
+                    rows = w.rearrange("(g t p) n -> g p t n", g=PASSES, t=PACK)
+                    nc.sync.dma_start(
+                        out=raw_slabs[(q, j)][:, g, :, :width], in_=rows[g][:, :, c0 : c0 + width]
+                    )
 
         def regroup(k):
-            s, g, c = pieces[k]
+            q, g, c, j = pieces[k]
             grouped = grouped_pool.tile([P, N_TILE, PACK], BF16, align_bytes=64)
             for copy, lo, hi in (
                 (nc.scalar.copy, 0, SCALAR_COLS),
@@ -78,12 +85,12 @@ def tile_transformerblock_pb_kernel(tc, x, ao, wo, bo, g2, w1, w3, out_0, out_1)
             ):
                 copy(
                     out=grouped[:, lo:hi, :].rearrange("p (c i) t -> p c t i", i=4),
-                    in_=raw_slabs[s][:, g, :, c + lo : c + hi].rearrange("p t (c i) -> p c t i", i=4),
+                    in_=raw_slabs[(q, j)][:, g, :, c + lo : c + hi].rearrange("p t (c i) -> p c t i", i=4),
                 )
             grouped_pieces[k] = grouped
-            last_of_slab = k + 1 == len(pieces) or pieces[k + 1][0] != s
-            if last_of_slab and s + RAW_BUFS < len(slabs):
-                load_slab(s + RAW_BUFS)
+            last_of_group = k + 1 == len(pieces) or pieces[k + 1][0] != q
+            if last_of_group and q + 2 < len(groups):
+                load_group(q + 2)
 
         def quantise(k):
             codes = mx_pool.tile([P, N_TILE], U32, name="codes%d" % k, align_bytes=64)
@@ -122,25 +129,25 @@ def tile_transformerblock_pb_kernel(tc, x, ao, wo, bo, g2, w1, w3, out_0, out_1)
                 in_=grouped_act[:].rearrange("p g r t -> p (g r t)"),
             )
 
-        def contract(acc, act_codes, act_scales, m, s, c):
-            for g in range(PASSES):
-                nc.tensor.matmul_mx(
-                    out=acc[:],
-                    lhsT=act_codes[:, m, g, :].bitcast(FP8X4),
-                    lhsT_scale=act_scales[:, m, g, :],
-                    rhs=piece_codes[(s, g, c)][:].bitcast(FP8X4),
-                    rhs_scale=piece_scales[(s, g, c)][:],
-                    start=(g == 0),
-                    stop=(g == PASSES - 1),
-                )
+        def one_pass(acc, act_codes, act_scales, m, q, g, c, j):
+            nc.tensor.matmul_mx(
+                out=acc[:],
+                lhsT=act_codes[:, m, g, :].bitcast(FP8X4),
+                lhsT_scale=act_scales[:, m, g, :],
+                rhs=piece_codes[(q, g, c, j)][:].bitcast(FP8X4),
+                rhs_scale=piece_scales[(q, g, c, j)][:],
+                start=(g == 0),
+                stop=(g == PASSES - 1),
+            )
 
+        vectors = const.tile([P, 2 * D], BF16)
+        nc.vector.memset(vectors[:].bitcast(I32), 0)
+        ones = const.tile([P, P], BF16)
+        nc.vector.memset(ones[:], 1.0)
         ident = const.tile([P, P], BF16)
         make_identity(nc, ident[:])
         eps = const.tile([P, 1], F32)
         nc.vector.memset(eps[:], EPS)
-        bo_all = const.tile([P, D], BF16)
-        g2_all = const.tile([P, D], BF16)
-        nc.scalar.dma_start(out=bo_all[:], in_=bo.partition_broadcast(P))
         warm = const.tile([P, 1], F32)
         nc.scalar.activation(out=warm[:], in_=eps[:], func=ACT.Sqrt)
 
@@ -148,11 +155,20 @@ def tile_transformerblock_pb_kernel(tc, x, ao, wo, bo, g2, w1, w3, out_0, out_1)
         x_sb = acts.tile([P, B, 2, D], BF16)
         for b in range(B):
             nc.sync.dma_start(out=a_sb[:, b].rearrange("p h i d -> p h (i d)"), in_=ao_rows[b])
+            if b == 0:
+                nc.sync.dma_start(out=vectors[0:1, :D], in_=bo.rearrange("(o d) -> o d", o=1))
+                nc.sync.dma_start(out=vectors[0:1, D:], in_=g2.rearrange("(o d) -> o d", o=1))
             nc.sync.dma_start(out=x_sb[:, b].rearrange("p i d -> p (i d)"), in_=x_rows[b])
-        load_slab(0)
-        nc.sync.dma_start(out=g2_all[:], in_=g2.partition_broadcast(P))
-        for s in range(1, RAW_BUFS):
-            load_slab(s)
+        load_group(0)
+        load_group(1)
+
+        spread = const.tile([P, 2 * D], BF16)
+        for c in range(0, 2 * D, N_TILE):
+            summed = psum.tile([P, N_TILE], F32, tag="bank")
+            nc.tensor.matmul(out=summed[:], lhsT=ones[:], rhs=vectors[:, c : c + N_TILE], start=True, stop=True)
+            nc.scalar.copy(out=spread[:, c : c + N_TILE], in_=summed[:])
+        bo_all = spread[:, :D]
+        g2_all = spread[:, D:]
 
         a_codes = acts.tile([P, len(token_tiles), PASSES, P], U32, align_bytes=64)
         a_scales = acts.tile([P, len(token_tiles), PASSES, P], U8, align_bytes=64)
@@ -161,21 +177,26 @@ def tile_transformerblock_pb_kernel(tc, x, ao, wo, bo, g2, w1, w3, out_0, out_1)
             grouped_a = group_words(transpose_blocks(lambda h: a_sb[:, b, h, i, :]))
             x1_m = acts.tile([P, D], F32, name="x1_%d" % m)
             x1.append(x1_m)
-            nc.vector.tensor_tensor(out=x1_m[:], in0=x_sb[:, b, i, :], in1=bo_all[:], op=ALU.add)
+            nc.vector.tensor_tensor(out=x1_m[:], in0=x_sb[:, b, i, :], in1=bo_all, op=ALU.add)
             quantise_tokens(grouped_a, a_codes[:, m], a_scales[:, m])
 
-        for k in range(wo_pieces + 2):
-            weight_step()
-
+        acc = {}
+        for g in range(PASSES):
+            for k in range(D // N_TILE + (1 if g == 0 else 0)):
+                weight_step()
+            for m in range(len(token_tiles)):
+                for c in range(0, D, N_TILE):
+                    if g == 0:
+                        acc[(m, c)] = psum.tile([P, N_TILE], F32, tag="bank", name="acc%d_%d" % (m, c))
+                    one_pass(acc[(m, c)], a_codes, a_scales, m, 0, g, c, 0)
+        weight_step()
         sum_sq = const.tile([P, len(token_tiles)], F32)
-        for m in range(len(token_tiles)):
+        for m, (b, i) in enumerate(token_tiles):
             for c in range(0, D, N_TILE):
-                acc = psum.tile([P, N_TILE], F32, tag="bank")
-                contract(acc, a_codes, a_scales, m, 0, c)
                 nc.vector.tensor_tensor(
-                    out=x1[m][:, c : c + N_TILE], in0=acc[:], in1=x1[m][:, c : c + N_TILE], op=ALU.add
+                    out=x1[m][:, c : c + N_TILE], in0=acc[(m, c)][:], in1=x1[m][:, c : c + N_TILE], op=ALU.add
                 )
-            weight_step()
+            nc.sync.dma_start(out=x1_rows[b, i], in_=x1[m][:])
             squares = work.tile([P, D], BF16)
             nc.scalar.activation(
                 out=squares[:], in_=x1[m][:], func=ACT.Square, accum_out=sum_sq[:, m : m + 1]
@@ -183,6 +204,7 @@ def tile_transformerblock_pb_kernel(tc, x, ao, wo, bo, g2, w1, w3, out_0, out_1)
 
         rms = const.tile([P, len(token_tiles)], F32)
         nc.scalar.activation(out=rms[:], in_=sum_sq[:], func=ACT.Sqrt, scale=1.0 / D, bias=eps[:])
+        weight_step()
         inv_rms = const.tile([P, len(token_tiles)], F32)
         nc.vector.reciprocal(out=inv_rms[:], in_=rms[:])
         n_codes = acts.tile([P, len(token_tiles), PASSES, P], U32, align_bytes=64)
@@ -195,7 +217,7 @@ def tile_transformerblock_pb_kernel(tc, x, ao, wo, bo, g2, w1, w3, out_0, out_1)
                     out=n_sb[:],
                     in0=x1[m][:],
                     scalar=inv_rms[:, m : m + 1],
-                    in1=g2_all[:],
+                    in1=g2_all,
                     op0=ALU.mult,
                     op1=ALU.mult,
                 )
@@ -206,21 +228,18 @@ def tile_transformerblock_pb_kernel(tc, x, ao, wo, bo, g2, w1, w3, out_0, out_1)
             if m > 0:
                 quantise_tokens(grouped_n[m - 1], n_codes[:, m - 1], n_scales[:, m - 1])
 
-        for m, (b, i) in enumerate(token_tiles):
-            nc.sync.dma_start(out=x1_rows[b, i], in_=x1[m][:])
-
-        for s1 in range(1, len(slabs), 2):
-            s3 = s1 + 1
-            c0, width = slabs[s1][1], slabs[s1][2]
-            for m, (b, i) in enumerate(token_tiles):
-                h_sb = out_pool.tile([P, SLAB_COLS], F32)
-                for c in range(0, width, N_TILE):
+        for q in range(1, len(groups)):
+            c0, width = groups[q][0][1], groups[q][0][2]
+            for c in range(0, width, N_TILE):
+                for m, (b, i) in enumerate(token_tiles):
                     u = psum.tile([P, N_TILE], F32, tag="bank")
                     v = psum.tile([P, N_TILE], F32, tag="bank")
-                    contract(u, n_codes, n_scales, m, s1, c)
-                    contract(v, n_codes, n_scales, m, s3, c)
+                    for j, bank in enumerate((u, v)):
+                        for g in range(PASSES):
+                            one_pass(bank, n_codes, n_scales, m, q, g, c, j)
                     gate = out_pool.tile([P, N_TILE], F32)
                     nc.scalar.activation(out=gate[:], in_=u[:], func=ACT.Silu)
                     weight_step()
-                    nc.vector.tensor_tensor(out=h_sb[:, c : c + N_TILE], in0=v[:], in1=gate[:], op=ALU.mult)
-                nc.sync.dma_start(out=h_rows[b, i][:, c0 : c0 + width], in_=h_sb[:, :width])
+                    h_sb = out_pool.tile([P, N_TILE], F32)
+                    nc.vector.tensor_tensor(out=h_sb[:], in0=v[:], in1=gate[:], op=ALU.mult)
+                    nc.sync.dma_start(out=h_rows[b, i][:, c0 + c : c0 + c + N_TILE], in_=h_sb[:])

@@ -20,7 +20,9 @@ PACK = 4
 K_PASS = P * PACK
 PASSES = D // K_PASS
 N_TILE = 512
+TAIL_TILE = 256
 SLAB_COLS = 1024
+H_BUFS = 8
 RAW_BUFS = 4
 SCALAR_COLS = 256
 
@@ -39,11 +41,12 @@ def tile_transformerblock_pb_kernel(tc, x, ao, wo, bo, g2, w1, w3, out_0, out_1)
     groups = [[(wo, 0, D)]]
     for c0 in range(0, F, SLAB_COLS):
         groups.append([(w, c0, min(SLAB_COLS, F - c0)) for w in (w1, w3)])
+    piece_cols = [N_TILE] * (len(groups) - 1) + [TAIL_TILE]
     pieces = [
         (q, g, c, j)
         for q in range(len(groups))
         for g in range(PASSES)
-        for c in range(0, groups[q][0][2], N_TILE)
+        for c in range(0, groups[q][0][2], piece_cols[q])
         for j in range(len(groups[q]))
     ]
 
@@ -56,7 +59,6 @@ def tile_transformerblock_pb_kernel(tc, x, ao, wo, bo, g2, w1, w3, out_0, out_1)
         work = ctx.enter_context(tc.tile_pool(name="work", bufs=2))
         out_pool = ctx.enter_context(tc.tile_pool(name="out", bufs=4))
         psum = ctx.enter_context(tc.psum_pool(name="psum", bufs=8))
-        ctx.enter_context(tc.manual_schedule())
 
         raw_slabs = {}
         grouped_pieces = {}
@@ -78,10 +80,12 @@ def tile_transformerblock_pb_kernel(tc, x, ao, wo, bo, g2, w1, w3, out_0, out_1)
 
         def regroup(k):
             q, g, c, j = pieces[k]
+            cols = piece_cols[q]
+            scalar_cols = cols * SCALAR_COLS // N_TILE
             grouped = grouped_pool.tile([P, N_TILE, PACK], BF16, align_bytes=64)
             for copy, lo, hi in (
-                (nc.scalar.copy, 0, SCALAR_COLS),
-                (nc.vector.tensor_copy, SCALAR_COLS, N_TILE),
+                (nc.scalar.copy, 0, scalar_cols),
+                (nc.vector.tensor_copy, scalar_cols, cols),
             ):
                 copy(
                     out=grouped[:, lo:hi, :].rearrange("p (c i) t -> p c t i", i=4),
@@ -93,12 +97,13 @@ def tile_transformerblock_pb_kernel(tc, x, ao, wo, bo, g2, w1, w3, out_0, out_1)
                 load_group(q + 2)
 
         def quantise(k):
-            codes = mx_pool.tile([P, N_TILE], U32, name="codes%d" % k, align_bytes=64)
-            scales = mx_pool.tile([P, N_TILE], U8, name="scales%d" % k, align_bytes=64)
+            cols = piece_cols[pieces[k][0]]
+            codes = mx_pool.tile([P, cols], U32, name="codes%d" % k, align_bytes=64)
+            scales = mx_pool.tile([P, cols], U8, name="scales%d" % k, align_bytes=64)
             nc.vector.quantize_mx(
                 out=codes[:].bitcast(FP8X4),
                 scales=scales[:],
-                in_=grouped_pieces[k][:].rearrange("p w t -> p (w t)"),
+                in_=grouped_pieces[k][:, :cols, :].rearrange("p w t -> p (w t)"),
             )
             piece_codes[pieces[k]] = codes
             piece_scales[pieces[k]] = scales
@@ -118,7 +123,7 @@ def tile_transformerblock_pb_kernel(tc, x, ao, wo, bo, g2, w1, w3, out_0, out_1)
             return flipped
 
         def group_words(flipped):
-            grouped_act = work.tile([P, PASSES, P, PACK], BF16, align_bytes=64)
+            grouped_act = work.tile([P, PASSES, P, PACK], BF16, align_bytes=64, bufs=len(token_tiles))
             nc.scalar.copy(out=grouped_act[:], in_=flipped[:].rearrange("p (g t) r -> p g r t", t=PACK))
             return grouped_act
 
@@ -162,23 +167,29 @@ def tile_transformerblock_pb_kernel(tc, x, ao, wo, bo, g2, w1, w3, out_0, out_1)
         load_group(0)
         load_group(1)
 
-        spread = const.tile([P, 2 * D], BF16)
+        summed = {}
         for c in range(0, 2 * D, N_TILE):
-            summed = psum.tile([P, N_TILE], F32, tag="bank")
-            nc.tensor.matmul(out=summed[:], lhsT=ones[:], rhs=vectors[:, c : c + N_TILE], start=True, stop=True)
-            nc.scalar.copy(out=spread[:, c : c + N_TILE], in_=summed[:])
-        bo_all = spread[:, :D]
-        g2_all = spread[:, D:]
+            summed[c] = psum.tile([P, N_TILE], F32, tag="bank", name="summed%d" % c)
+            nc.tensor.matmul(
+                out=summed[c][:], lhsT=ones[:], rhs=vectors[:, c : c + N_TILE], start=True, stop=True
+            )
 
-        a_codes = acts.tile([P, len(token_tiles), PASSES, P], U32, align_bytes=64)
-        a_scales = acts.tile([P, len(token_tiles), PASSES, P], U8, align_bytes=64)
         x1 = []
         for m, (b, i) in enumerate(token_tiles):
-            grouped_a = group_words(transpose_blocks(lambda h: a_sb[:, b, h, i, :]))
             x1_m = acts.tile([P, D], F32, name="x1_%d" % m)
             x1.append(x1_m)
-            nc.vector.tensor_tensor(out=x1_m[:], in0=x_sb[:, b, i, :], in1=bo_all, op=ALU.add)
+            for c in range(0, D, N_TILE):
+                nc.vector.tensor_tensor(
+                    out=x1_m[:, c : c + N_TILE], in0=summed[c][:], in1=x_sb[:, b, i, c : c + N_TILE], op=ALU.add
+                )
+        a_codes = acts.tile([P, len(token_tiles), PASSES, P], U32, align_bytes=64)
+        a_scales = acts.tile([P, len(token_tiles), PASSES, P], U8, align_bytes=64)
+        for m, (b, i) in enumerate(token_tiles):
+            grouped_a = group_words(transpose_blocks(lambda h: a_sb[:, b, h, i, :]))
             quantise_tokens(grouped_a, a_codes[:, m], a_scales[:, m])
+        g2_all = const.tile([P, D], BF16)
+        for c in range(0, D, N_TILE):
+            nc.scalar.copy(out=g2_all[:, c : c + N_TILE], in_=summed[D + c][:])
 
         acc = {}
         for g in range(PASSES):
@@ -217,7 +228,7 @@ def tile_transformerblock_pb_kernel(tc, x, ao, wo, bo, g2, w1, w3, out_0, out_1)
                     out=n_sb[:],
                     in0=x1[m][:],
                     scalar=inv_rms[:, m : m + 1],
-                    in1=g2_all,
+                    in1=g2_all[:],
                     op0=ALU.mult,
                     op1=ALU.mult,
                 )
@@ -230,16 +241,17 @@ def tile_transformerblock_pb_kernel(tc, x, ao, wo, bo, g2, w1, w3, out_0, out_1)
 
         for q in range(1, len(groups)):
             c0, width = groups[q][0][1], groups[q][0][2]
-            for c in range(0, width, N_TILE):
+            cols = piece_cols[q]
+            for c in range(0, width, cols):
                 for m, (b, i) in enumerate(token_tiles):
-                    u = psum.tile([P, N_TILE], F32, tag="bank")
-                    v = psum.tile([P, N_TILE], F32, tag="bank")
+                    u = psum.tile([P, cols], F32, tag="bank")
+                    v = psum.tile([P, cols], F32, tag="bank")
                     for j, bank in enumerate((u, v)):
                         for g in range(PASSES):
                             one_pass(bank, n_codes, n_scales, m, q, g, c, j)
-                    gate = out_pool.tile([P, N_TILE], F32)
+                    gate = out_pool.tile([P, cols], F32)
                     nc.scalar.activation(out=gate[:], in_=u[:], func=ACT.Silu)
                     weight_step()
-                    h_sb = out_pool.tile([P, N_TILE], F32)
+                    h_sb = out_pool.tile([P, cols], F32, bufs=H_BUFS)
                     nc.vector.tensor_tensor(out=h_sb[:], in0=v[:], in1=gate[:], op=ALU.mult)
-                    nc.sync.dma_start(out=h_rows[b, i][:, c0 + c : c0 + c + N_TILE], in_=h_sb[:])
+                    nc.sync.dma_start(out=h_rows[b, i][:, c0 + c : c0 + c + cols], in_=h_sb[:])

@@ -24,9 +24,13 @@ TAIL_TILE = 256
 SLAB_COLS = 1024
 H_BUFS = 8
 RAW_BUFS = 4
-SCALAR_COLS = 256
+TENSOR_COLS = 176
+SCALAR_COLS = 144
+ACC_BANKS = 6
+MOVED_BANKS = 2
 
 FLOPS = 2 * B * S * D * (D + 2 * F)
+assert 2 * P * (D * (D + 2 * F) * TENSOR_COLS // N_TILE + P * 2 * D) <= FLOPS // 10
 
 
 def tile_transformerblock_pb_kernel(tc, x, ao, wo, bo, g2, w1, w3, out_0, out_1):
@@ -34,7 +38,7 @@ def tile_transformerblock_pb_kernel(tc, x, ao, wo, bo, g2, w1, w3, out_0, out_1)
 
     token_tiles = [(b, i) for b in range(B) for i in range(2)]
     ao_rows = ao.rearrange("b h (p i) d -> b p h (i d)", i=2)
-    x_rows = x.rearrange("b (p i) d -> b p (i d)", i=2)
+    x_rows = x.rearrange("b (p i) d -> b i p d", i=2)
     x1_rows = out_0.rearrange("b (p i) d -> b i p d", i=2)
     h_rows = out_1.rearrange("b (p i) f -> b i p f", i=2)
 
@@ -58,7 +62,8 @@ def tile_transformerblock_pb_kernel(tc, x, ao, wo, bo, g2, w1, w3, out_0, out_1)
         mx_pool = ctx.enter_context(tc.tile_pool(name="mx", bufs=1))
         work = ctx.enter_context(tc.tile_pool(name="work", bufs=2))
         out_pool = ctx.enter_context(tc.tile_pool(name="out", bufs=4))
-        psum = ctx.enter_context(tc.psum_pool(name="psum", bufs=8))
+        psum = ctx.enter_context(tc.psum_pool(name="psum", bufs=ACC_BANKS))
+        moved_pool = ctx.enter_context(tc.psum_pool(name="moved", bufs=MOVED_BANKS))
 
         raw_slabs = {}
         grouped_pieces = {}
@@ -81,15 +86,27 @@ def tile_transformerblock_pb_kernel(tc, x, ao, wo, bo, g2, w1, w3, out_0, out_1)
         def regroup(k):
             q, g, c, j = pieces[k]
             cols = piece_cols[q]
-            scalar_cols = cols * SCALAR_COLS // N_TILE
+            tensor_cols = cols * TENSOR_COLS // N_TILE
+            scalar_end = tensor_cols + cols * SCALAR_COLS // N_TILE
+            piece_rows = raw_slabs[(q, j)][:, g, :, c : c + cols]
             grouped = grouped_pool.tile([P, N_TILE, PACK], BF16, align_bytes=64)
+            moved = moved_pool.tile([P, N_TILE // 2, PACK], BF16)
+            for t in range(0, PACK, 2):
+                nc.tensor.matmul(
+                    out=moved[:, :tensor_cols, t : t + 2].rearrange("p c t -> p t c"),
+                    lhsT=ident[:],
+                    rhs=piece_rows[:, t : t + 2, :tensor_cols],
+                    start=True,
+                    stop=True,
+                )
+            nc.scalar.copy(out=grouped[:, :tensor_cols, :], in_=moved[:, :tensor_cols, :])
             for copy, lo, hi in (
-                (nc.scalar.copy, 0, scalar_cols),
-                (nc.vector.tensor_copy, scalar_cols, cols),
+                (nc.scalar.copy, tensor_cols, scalar_end),
+                (nc.vector.tensor_copy, scalar_end, cols),
             ):
                 copy(
                     out=grouped[:, lo:hi, :].rearrange("p (c i) t -> p c t i", i=4),
-                    in_=raw_slabs[(q, j)][:, g, :, c + lo : c + hi].rearrange("p t (c i) -> p c t i", i=4),
+                    in_=piece_rows[:, :, lo:hi].rearrange("p t (c i) -> p c t i", i=4),
                 )
             grouped_pieces[k] = grouped
             last_of_group = k + 1 == len(pieces) or pieces[k + 1][0] != q
@@ -116,15 +133,13 @@ def tile_transformerblock_pb_kernel(tc, x, ao, wo, bo, g2, w1, w3, out_0, out_1)
                 quantise(k - 1)
             progress["steps"] = k + 1
 
-        def transpose_blocks(rows_of):
-            flipped = psum.tile([P, PASSES * PACK, P], BF16, tag="bank")
-            for c in range(PASSES * PACK):
-                nc.tensor.transpose(out=flipped[:, c, :], in_=rows_of(c), identity=ident[:])
-            return flipped
-
-        def group_words(flipped):
+        def transpose_and_group(rows_of):
             grouped_act = work.tile([P, PASSES, P, PACK], BF16, align_bytes=64, bufs=len(token_tiles))
-            nc.scalar.copy(out=grouped_act[:], in_=flipped[:].rearrange("p (g t) r -> p g r t", t=PACK))
+            for g in range(PASSES):
+                flipped = psum.tile([P, PACK, P], BF16, tag="bank")
+                for t in range(PACK):
+                    nc.tensor.transpose(out=flipped[:, t, :], in_=rows_of(g * PACK + t), identity=ident[:])
+                nc.scalar.copy(out=grouped_act[:, g], in_=flipped[:].rearrange("p t r -> p r t"))
             return grouped_act
 
         def quantise_tokens(grouped_act, codes, scales):
@@ -159,21 +174,32 @@ def tile_transformerblock_pb_kernel(tc, x, ao, wo, bo, g2, w1, w3, out_0, out_1)
         a_sb = acts.tile([P, B, H, 2, DK], BF16)
         x_sb = acts.tile([P, B, 2, D], BF16)
         for b in range(B):
-            nc.sync.dma_start(out=a_sb[:, b].rearrange("p h i d -> p h (i d)"), in_=ao_rows[b])
-            if b == 0:
-                nc.sync.dma_start(out=vectors[0:1, :D], in_=bo.rearrange("(o d) -> o d", o=1))
-                nc.sync.dma_start(out=vectors[0:1, D:], in_=g2.rearrange("(o d) -> o d", o=1))
-            nc.sync.dma_start(out=x_sb[:, b].rearrange("p i d -> p (i d)"), in_=x_rows[b])
+            for half in range(2):
+                heads = slice(half * PACK, (half + 1) * PACK)
+                nc.sync.dma_start(
+                    out=a_sb[:, b, heads].rearrange("p h i d -> p h (i d)"), in_=ao_rows[b][:, heads, :]
+                )
+                if (b, half) == (0, 0):
+                    nc.sync.dma_start(out=vectors[0:1, :D], in_=bo.rearrange("(o d) -> o d", o=1))
+                    nc.sync.dma_start(out=vectors[0:1, D:], in_=g2.rearrange("(o d) -> o d", o=1))
+                nc.sync.dma_start(out=x_sb[:, b, half, :], in_=x_rows[b, half])
         load_group(0)
         load_group(1)
 
-        summed = {}
-        for c in range(0, 2 * D, N_TILE):
-            summed[c] = psum.tile([P, N_TILE], F32, tag="bank", name="summed%d" % c)
-            nc.tensor.matmul(
-                out=summed[c][:], lhsT=ones[:], rhs=vectors[:, c : c + N_TILE], start=True, stop=True
-            )
+        def spread(first):
+            banks = {}
+            for c in range(0, D, N_TILE):
+                banks[c] = psum.tile([P, N_TILE], F32, tag="bank", name="spread%d" % (first + c))
+                nc.tensor.matmul(
+                    out=banks[c][:],
+                    lhsT=ones[:],
+                    rhs=vectors[:, first + c : first + c + N_TILE],
+                    start=True,
+                    stop=True,
+                )
+            return banks
 
+        summed = spread(0)
         x1 = []
         for m, (b, i) in enumerate(token_tiles):
             x1_m = acts.tile([P, D], F32, name="x1_%d" % m)
@@ -185,27 +211,20 @@ def tile_transformerblock_pb_kernel(tc, x, ao, wo, bo, g2, w1, w3, out_0, out_1)
         a_codes = acts.tile([P, len(token_tiles), PASSES, P], U32, align_bytes=64)
         a_scales = acts.tile([P, len(token_tiles), PASSES, P], U8, align_bytes=64)
         for m, (b, i) in enumerate(token_tiles):
-            grouped_a = group_words(transpose_blocks(lambda h: a_sb[:, b, h, i, :]))
+            grouped_a = transpose_and_group(lambda h: a_sb[:, b, h, i, :])
             quantise_tokens(grouped_a, a_codes[:, m], a_scales[:, m])
-        g2_all = const.tile([P, D], BF16)
-        for c in range(0, D, N_TILE):
-            nc.scalar.copy(out=g2_all[:, c : c + N_TILE], in_=summed[D + c][:])
 
-        acc = {}
-        for g in range(PASSES):
-            for k in range(D // N_TILE + (1 if g == 0 else 0)):
-                weight_step()
-            for m in range(len(token_tiles)):
-                for c in range(0, D, N_TILE):
-                    if g == 0:
-                        acc[(m, c)] = psum.tile([P, N_TILE], F32, tag="bank", name="acc%d_%d" % (m, c))
-                    one_pass(acc[(m, c)], a_codes, a_scales, m, 0, g, c, 0)
-        weight_step()
+        wo_pieces = sum(1 for piece in pieces if piece[0] == 0)
+        for k in range(wo_pieces + 1):
+            weight_step()
         sum_sq = const.tile([P, len(token_tiles)], F32)
         for m, (b, i) in enumerate(token_tiles):
             for c in range(0, D, N_TILE):
+                acc = psum.tile([P, N_TILE], F32, tag="bank")
+                for g in range(PASSES):
+                    one_pass(acc, a_codes, a_scales, m, 0, g, c, 0)
                 nc.vector.tensor_tensor(
-                    out=x1[m][:, c : c + N_TILE], in0=acc[(m, c)][:], in1=x1[m][:, c : c + N_TILE], op=ALU.add
+                    out=x1[m][:, c : c + N_TILE], in0=acc[:], in1=x1[m][:, c : c + N_TILE], op=ALU.add
                 )
             nc.sync.dma_start(out=x1_rows[b, i], in_=x1[m][:])
             squares = work.tile([P, D], BF16)
@@ -215,29 +234,28 @@ def tile_transformerblock_pb_kernel(tc, x, ao, wo, bo, g2, w1, w3, out_0, out_1)
 
         rms = const.tile([P, len(token_tiles)], F32)
         nc.scalar.activation(out=rms[:], in_=sum_sq[:], func=ACT.Sqrt, scale=1.0 / D, bias=eps[:])
-        weight_step()
+        for k in range(2):
+            weight_step()
         inv_rms = const.tile([P, len(token_tiles)], F32)
         nc.vector.reciprocal(out=inv_rms[:], in_=rms[:])
         n_codes = acts.tile([P, len(token_tiles), PASSES, P], U32, align_bytes=64)
         n_scales = acts.tile([P, len(token_tiles), PASSES, P], U8, align_bytes=64)
-        grouped_n = {}
-        for m in range(len(token_tiles) + 1):
-            if m < len(token_tiles):
-                n_sb = work.tile([P, D], BF16)
+        g2_all = spread(D)
+        for m in range(len(token_tiles)):
+            n_sb = work.tile([P, D], BF16)
+            for c in range(0, D, N_TILE):
                 nc.vector.scalar_tensor_tensor(
-                    out=n_sb[:],
-                    in0=x1[m][:],
+                    out=n_sb[:, c : c + N_TILE],
+                    in0=x1[m][:, c : c + N_TILE],
                     scalar=inv_rms[:, m : m + 1],
-                    in1=g2_all[:],
+                    in1=g2_all[c][:],
                     op0=ALU.mult,
                     op1=ALU.mult,
                 )
-                flipped_n = transpose_blocks(lambda c: n_sb[:, c * P : (c + 1) * P])
+            grouped_n = transpose_and_group(lambda c: n_sb[:, c * P : (c + 1) * P])
             weight_step()
-            if m < len(token_tiles):
-                grouped_n[m] = group_words(flipped_n)
-            if m > 0:
-                quantise_tokens(grouped_n[m - 1], n_codes[:, m - 1], n_scales[:, m - 1])
+            quantise_tokens(grouped_n, n_codes[:, m], n_scales[:, m])
+        weight_step()
 
         for q in range(1, len(groups)):
             c0, width = groups[q][0][1], groups[q][0][2]

@@ -7,7 +7,6 @@ F32 = mybir.dt.float32
 BF16 = mybir.dt.bfloat16
 U32 = mybir.dt.uint32
 U8 = mybir.dt.uint8
-I32 = mybir.dt.int32
 FP8X4 = mybir.dt.float8_e4m3fn_x4
 ACT = mybir.ActivationFunctionType
 ALU = mybir.AluOpType
@@ -24,13 +23,9 @@ TAIL_TILE = 256
 SLAB_COLS = 1024
 H_BUFS = 8
 RAW_BUFS = 4
-TENSOR_COLS = 176
-SCALAR_COLS = 144
-ACC_BANKS = 6
-MOVED_BANKS = 2
+SCALAR_COLS = 272
 
 FLOPS = 2 * B * S * D * (D + 2 * F)
-assert 2 * P * (D * (D + 2 * F) * TENSOR_COLS // N_TILE + P * 2 * D) <= FLOPS // 10
 
 
 def tile_transformerblock_pb_kernel(tc, x, ao, wo, bo, g2, w1, w3, out_0, out_1):
@@ -62,8 +57,7 @@ def tile_transformerblock_pb_kernel(tc, x, ao, wo, bo, g2, w1, w3, out_0, out_1)
         mx_pool = ctx.enter_context(tc.tile_pool(name="mx", bufs=1))
         work = ctx.enter_context(tc.tile_pool(name="work", bufs=2))
         out_pool = ctx.enter_context(tc.tile_pool(name="out", bufs=4))
-        psum = ctx.enter_context(tc.psum_pool(name="psum", bufs=ACC_BANKS))
-        moved_pool = ctx.enter_context(tc.psum_pool(name="moved", bufs=MOVED_BANKS))
+        psum = ctx.enter_context(tc.psum_pool(name="psum", bufs=8))
 
         raw_slabs = {}
         grouped_pieces = {}
@@ -86,27 +80,15 @@ def tile_transformerblock_pb_kernel(tc, x, ao, wo, bo, g2, w1, w3, out_0, out_1)
         def regroup(k):
             q, g, c, j = pieces[k]
             cols = piece_cols[q]
-            tensor_cols = cols * TENSOR_COLS // N_TILE
-            scalar_end = tensor_cols + cols * SCALAR_COLS // N_TILE
-            piece_rows = raw_slabs[(q, j)][:, g, :, c : c + cols]
+            scalar_cols = cols * SCALAR_COLS // N_TILE
             grouped = grouped_pool.tile([P, N_TILE, PACK], BF16, align_bytes=64)
-            moved = moved_pool.tile([P, N_TILE // 2, PACK], BF16)
-            for t in range(0, PACK, 2):
-                nc.tensor.matmul(
-                    out=moved[:, :tensor_cols, t : t + 2].rearrange("p c t -> p t c"),
-                    lhsT=ident[:],
-                    rhs=piece_rows[:, t : t + 2, :tensor_cols],
-                    start=True,
-                    stop=True,
-                )
-            nc.scalar.copy(out=grouped[:, :tensor_cols, :], in_=moved[:, :tensor_cols, :])
             for copy, lo, hi in (
-                (nc.scalar.copy, tensor_cols, scalar_end),
-                (nc.vector.tensor_copy, scalar_end, cols),
+                (nc.scalar.copy, 0, scalar_cols),
+                (nc.vector.tensor_copy, scalar_cols, cols),
             ):
                 copy(
                     out=grouped[:, lo:hi, :].rearrange("p (c i) t -> p c t i", i=4),
-                    in_=piece_rows[:, :, lo:hi].rearrange("p t (c i) -> p c t i", i=4),
+                    in_=raw_slabs[(q, j)][:, g, :, c + lo : c + hi].rearrange("p t (c i) -> p c t i", i=4),
                 )
             grouped_pieces[k] = grouped
             last_of_group = k + 1 == len(pieces) or pieces[k + 1][0] != q
@@ -160,8 +142,10 @@ def tile_transformerblock_pb_kernel(tc, x, ao, wo, bo, g2, w1, w3, out_0, out_1)
                 stop=(g == PASSES - 1),
             )
 
-        vectors = const.tile([P, 2 * D], BF16)
-        nc.vector.memset(vectors[:].bitcast(I32), 0)
+        bo_row = const.tile([P, D], BF16)
+        nc.gpsimd.memset(bo_row[:].bitcast(F32), 0.0)
+        g2_row = const.tile([P, D], BF16)
+        nc.gpsimd.memset(g2_row[:].bitcast(F32), 0.0)
         ones = const.tile([P, P], BF16)
         nc.vector.memset(ones[:], 1.0)
         ident = const.tile([P, P], BF16)
@@ -171,42 +155,37 @@ def tile_transformerblock_pb_kernel(tc, x, ao, wo, bo, g2, w1, w3, out_0, out_1)
         warm = const.tile([P, 1], F32)
         nc.scalar.activation(out=warm[:], in_=eps[:], func=ACT.Sqrt)
 
+        nc.sync.dma_start(out=bo_row[0:1, :], in_=bo.rearrange("(o d) -> o d", o=1))
         a_sb = acts.tile([P, B, H, 2, DK], BF16)
         x_sb = acts.tile([P, B, 2, D], BF16)
         for b in range(B):
-            for half in range(2):
-                heads = slice(half * PACK, (half + 1) * PACK)
+            for part in range(2):
+                heads = slice(part * PACK, (part + 1) * PACK)
                 nc.sync.dma_start(
                     out=a_sb[:, b, heads].rearrange("p h i d -> p h (i d)"), in_=ao_rows[b][:, heads, :]
                 )
-                if (b, half) == (0, 0):
-                    nc.sync.dma_start(out=vectors[0:1, :D], in_=bo.rearrange("(o d) -> o d", o=1))
-                    nc.sync.dma_start(out=vectors[0:1, D:], in_=g2.rearrange("(o d) -> o d", o=1))
-                nc.sync.dma_start(out=x_sb[:, b, half, :], in_=x_rows[b, half])
+                nc.sync.dma_start(out=x_sb[:, b, part, :], in_=x_rows[b, part])
+        nc.sync.dma_start(out=g2_row[0:1, :], in_=g2.rearrange("(o d) -> o d", o=1))
         load_group(0)
         load_group(1)
 
-        def spread(first):
+        def spread(vector_row, name):
             banks = {}
             for c in range(0, D, N_TILE):
-                banks[c] = psum.tile([P, N_TILE], F32, tag="bank", name="spread%d" % (first + c))
+                banks[c] = psum.tile([P, N_TILE], F32, tag="bank", name="%s%d" % (name, c))
                 nc.tensor.matmul(
-                    out=banks[c][:],
-                    lhsT=ones[:],
-                    rhs=vectors[:, first + c : first + c + N_TILE],
-                    start=True,
-                    stop=True,
+                    out=banks[c][:], lhsT=ones[:], rhs=vector_row[:, c : c + N_TILE], start=True, stop=True
                 )
             return banks
 
-        summed = spread(0)
+        bo_all = spread(bo_row, "bo_all")
         x1 = []
         for m, (b, i) in enumerate(token_tiles):
             x1_m = acts.tile([P, D], F32, name="x1_%d" % m)
             x1.append(x1_m)
             for c in range(0, D, N_TILE):
                 nc.vector.tensor_tensor(
-                    out=x1_m[:, c : c + N_TILE], in0=summed[c][:], in1=x_sb[:, b, i, c : c + N_TILE], op=ALU.add
+                    out=x1_m[:, c : c + N_TILE], in0=bo_all[c][:], in1=x_sb[:, b, i, c : c + N_TILE], op=ALU.add
                 )
         a_codes = acts.tile([P, len(token_tiles), PASSES, P], U32, align_bytes=64)
         a_scales = acts.tile([P, len(token_tiles), PASSES, P], U8, align_bytes=64)
@@ -214,17 +193,21 @@ def tile_transformerblock_pb_kernel(tc, x, ao, wo, bo, g2, w1, w3, out_0, out_1)
             grouped_a = transpose_and_group(lambda h: a_sb[:, b, h, i, :])
             quantise_tokens(grouped_a, a_codes[:, m], a_scales[:, m])
 
-        wo_pieces = sum(1 for piece in pieces if piece[0] == 0)
-        for k in range(wo_pieces + 1):
-            weight_step()
+        acc = {}
+        for g in range(PASSES):
+            for k in range(D // N_TILE + (1 if g == 0 else 0)):
+                weight_step()
+            for m in range(len(token_tiles)):
+                for c in range(0, D, N_TILE):
+                    if g == 0:
+                        acc[(m, c)] = psum.tile([P, N_TILE], F32, tag="bank", name="acc%d_%d" % (m, c))
+                    one_pass(acc[(m, c)], a_codes, a_scales, m, 0, g, c, 0)
+        weight_step()
         sum_sq = const.tile([P, len(token_tiles)], F32)
         for m, (b, i) in enumerate(token_tiles):
             for c in range(0, D, N_TILE):
-                acc = psum.tile([P, N_TILE], F32, tag="bank")
-                for g in range(PASSES):
-                    one_pass(acc, a_codes, a_scales, m, 0, g, c, 0)
                 nc.vector.tensor_tensor(
-                    out=x1[m][:, c : c + N_TILE], in0=acc[:], in1=x1[m][:, c : c + N_TILE], op=ALU.add
+                    out=x1[m][:, c : c + N_TILE], in0=acc[(m, c)][:], in1=x1[m][:, c : c + N_TILE], op=ALU.add
                 )
             nc.sync.dma_start(out=x1_rows[b, i], in_=x1[m][:])
             squares = work.tile([P, D], BF16)
@@ -234,13 +217,12 @@ def tile_transformerblock_pb_kernel(tc, x, ao, wo, bo, g2, w1, w3, out_0, out_1)
 
         rms = const.tile([P, len(token_tiles)], F32)
         nc.scalar.activation(out=rms[:], in_=sum_sq[:], func=ACT.Sqrt, scale=1.0 / D, bias=eps[:])
-        for k in range(2):
-            weight_step()
+        weight_step()
         inv_rms = const.tile([P, len(token_tiles)], F32)
         nc.vector.reciprocal(out=inv_rms[:], in_=rms[:])
         n_codes = acts.tile([P, len(token_tiles), PASSES, P], U32, align_bytes=64)
         n_scales = acts.tile([P, len(token_tiles), PASSES, P], U8, align_bytes=64)
-        g2_all = spread(D)
+        g2_all = spread(g2_row, "g2_all")
         for m in range(len(token_tiles)):
             n_sb = work.tile([P, D], BF16)
             for c in range(0, D, N_TILE):

from contextlib import ExitStack

import concourse.mybir as mybir
from concourse.masks import make_identity

F32 = mybir.dt.float32
BF16 = mybir.dt.bfloat16
U32 = mybir.dt.uint32
U8 = mybir.dt.uint8
FP8X4 = mybir.dt.float8_e4m3fn_x4
ACT = mybir.ActivationFunctionType
ALU = mybir.AluOpType

B, S, D, H, DK, F = 2, 256, 1024, 8, 128, 2560
EPS = 1e-6

P = 128
PACK = 4
K_PASS = P * PACK
PASSES = D // K_PASS
N_TILE = 512
TAIL_TILE = 256
SLAB_COLS = 1024
H_BUFS = 8
RAW_BUFS = 4
SCALAR_COLS = 272

FLOPS = 2 * B * S * D * (D + 2 * F)


def tile_transformerblock_pb_kernel(tc, x, ao, wo, bo, g2, w1, w3, out_0, out_1):
    nc = tc.nc

    token_tiles = [(b, i) for b in range(B) for i in range(2)]
    ao_rows = ao.rearrange("b h (p i) d -> b p h (i d)", i=2)
    x_rows = x.rearrange("b (p i) d -> b i p d", i=2)
    x1_rows = out_0.rearrange("b (p i) d -> b i p d", i=2)
    h_rows = out_1.rearrange("b (p i) f -> b i p f", i=2)

    groups = [[(wo, 0, D)]]
    for c0 in range(0, F, SLAB_COLS):
        groups.append([(w, c0, min(SLAB_COLS, F - c0)) for w in (w1, w3)])
    piece_cols = [N_TILE] * (len(groups) - 1) + [TAIL_TILE]
    pieces = [
        (q, g, c, j)
        for q in range(len(groups))
        for g in range(PASSES)
        for c in range(0, groups[q][0][2], piece_cols[q])
        for j in range(len(groups[q]))
    ]

    with ExitStack() as ctx:
        const = ctx.enter_context(tc.tile_pool(name="const", bufs=1))
        acts = ctx.enter_context(tc.tile_pool(name="acts", bufs=1))
        raw_pool = ctx.enter_context(tc.tile_pool(name="raw", bufs=RAW_BUFS))
        grouped_pool = ctx.enter_context(tc.tile_pool(name="grouped", bufs=4))
        mx_pool = ctx.enter_context(tc.tile_pool(name="mx", bufs=1))
        work = ctx.enter_context(tc.tile_pool(name="work", bufs=2))
        out_pool = ctx.enter_context(tc.tile_pool(name="out", bufs=4))
        psum = ctx.enter_context(tc.psum_pool(name="psum", bufs=8))

        raw_slabs = {}
        grouped_pieces = {}
        piece_codes = {}
        piece_scales = {}
        progress = {"steps": 0}

        def load_group(q):
            for j in range(len(groups[q])):
                raw_slabs[(q, j)] = raw_pool.tile(
                    [P, PASSES, PACK, SLAB_COLS], BF16, tag="raw", name="raw%d_%d" % (q, j)
                )
            for g in range(PASSES):
                for j, (w, c0, width) in enumerate(groups[q]):
                    rows = w.rearrange("(g t p) n -> g p t n", g=PASSES, t=PACK)
                    nc.sync.dma_start(
                        out=raw_slabs[(q, j)][:, g, :, :width], in_=rows[g][:, :, c0 : c0 + width]
                    )

        def regroup(k):
            q, g, c, j = pieces[k]
            cols = piece_cols[q]
            scalar_cols = cols * SCALAR_COLS // N_TILE
            grouped = grouped_pool.tile([P, N_TILE, PACK], BF16, align_bytes=64)
            for copy, lo, hi in (
                (nc.scalar.copy, 0, scalar_cols),
                (nc.vector.tensor_copy, scalar_cols, cols),
            ):
                copy(
                    out=grouped[:, lo:hi, :].rearrange("p (c i) t -> p c t i", i=4),
                    in_=raw_slabs[(q, j)][:, g, :, c + lo : c + hi].rearrange("p t (c i) -> p c t i", i=4),
                )
            grouped_pieces[k] = grouped
            last_of_group = k + 1 == len(pieces) or pieces[k + 1][0] != q
            if last_of_group and q + 2 < len(groups):
                load_group(q + 2)

        def quantise(k):
            cols = piece_cols[pieces[k][0]]
            codes = mx_pool.tile([P, cols], U32, name="codes%d" % k, align_bytes=64)
            scales = mx_pool.tile([P, cols], U8, name="scales%d" % k, align_bytes=64)
            nc.vector.quantize_mx(
                out=codes[:].bitcast(FP8X4),
                scales=scales[:],
                in_=grouped_pieces[k][:, :cols, :].rearrange("p w t -> p (w t)"),
            )
            piece_codes[pieces[k]] = codes
            piece_scales[pieces[k]] = scales

        def weight_step():
            k = progress["steps"]
            if k < len(pieces):
                regroup(k)
            if 1 <= k <= len(pieces):
                quantise(k - 1)
            progress["steps"] = k + 1

        def transpose_and_group(rows_of):
            grouped_act = work.tile([P, PASSES, P, PACK], BF16, align_bytes=64, bufs=len(token_tiles))
            for g in range(PASSES):
                flipped = psum.tile([P, PACK, P], BF16, tag="bank")
                for t in range(PACK):
                    nc.tensor.transpose(out=flipped[:, t, :], in_=rows_of(g * PACK + t), identity=ident[:])
                nc.scalar.copy(out=grouped_act[:, g], in_=flipped[:].rearrange("p t r -> p r t"))
            return grouped_act

        def quantise_tokens(grouped_act, codes, scales):
            nc.vector.quantize_mx(
                out=codes.rearrange("p g r -> p (g r)").bitcast(FP8X4),
                scales=scales.rearrange("p g r -> p (g r)"),
                in_=grouped_act[:].rearrange("p g r t -> p (g r t)"),
            )

        def one_pass(acc, act_codes, act_scales, m, q, g, c, j):
            nc.tensor.matmul_mx(
                out=acc[:],
                lhsT=act_codes[:, m, g, :].bitcast(FP8X4),
                lhsT_scale=act_scales[:, m, g, :],
                rhs=piece_codes[(q, g, c, j)][:].bitcast(FP8X4),
                rhs_scale=piece_scales[(q, g, c, j)][:],
                start=(g == 0),
                stop=(g == PASSES - 1),
            )

        bo_row = const.tile([P, D], BF16)
        nc.gpsimd.memset(bo_row[:].bitcast(F32), 0.0)
        g2_row = const.tile([P, D], BF16)
        nc.gpsimd.memset(g2_row[:].bitcast(F32), 0.0)
        ones = const.tile([P, P], BF16)
        nc.vector.memset(ones[:], 1.0)
        ident = const.tile([P, P], BF16)
        make_identity(nc, ident[:])
        eps = const.tile([P, 1], F32)
        nc.vector.memset(eps[:], EPS)
        warm = const.tile([P, 1], F32)
        nc.scalar.activation(out=warm[:], in_=eps[:], func=ACT.Sqrt)

        nc.sync.dma_start(out=bo_row[0:1, :], in_=bo.rearrange("(o d) -> o d", o=1))
        a_sb = acts.tile([P, B, H, 2, DK], BF16)
        x_sb = acts.tile([P, B, 2, D], BF16)
        for b in range(B):
            for part in range(2):
                heads = slice(part * PACK, (part + 1) * PACK)
                nc.sync.dma_start(
                    out=a_sb[:, b, heads].rearrange("p h i d -> p h (i d)"), in_=ao_rows[b][:, heads, :]
                )
                nc.sync.dma_start(out=x_sb[:, b, part, :], in_=x_rows[b, part])
        nc.sync.dma_start(out=g2_row[0:1, :], in_=g2.rearrange("(o d) -> o d", o=1))
        load_group(0)
        load_group(1)

        def spread(vector_row, name):
            banks = {}
            for c in range(0, D, N_TILE):
                banks[c] = psum.tile([P, N_TILE], F32, tag="bank", name="%s%d" % (name, c))
                nc.tensor.matmul(
                    out=banks[c][:], lhsT=ones[:], rhs=vector_row[:, c : c + N_TILE], start=True, stop=True
                )
            return banks

        bo_all = spread(bo_row, "bo_all")
        x1 = []
        for m, (b, i) in enumerate(token_tiles):
            x1_m = acts.tile([P, D], F32, name="x1_%d" % m)
            x1.append(x1_m)
            for c in range(0, D, N_TILE):
                nc.vector.tensor_tensor(
                    out=x1_m[:, c : c + N_TILE], in0=bo_all[c][:], in1=x_sb[:, b, i, c : c + N_TILE], op=ALU.add
                )
        a_codes = acts.tile([P, len(token_tiles), PASSES, P], U32, align_bytes=64)
        a_scales = acts.tile([P, len(token_tiles), PASSES, P], U8, align_bytes=64)
        for m, (b, i) in enumerate(token_tiles):
            grouped_a = transpose_and_group(lambda h: a_sb[:, b, h, i, :])
            quantise_tokens(grouped_a, a_codes[:, m], a_scales[:, m])

        acc = {}
        for g in range(PASSES):
            for k in range(D // N_TILE + (1 if g == 0 else 0)):
                weight_step()
            for m in range(len(token_tiles)):
                for c in range(0, D, N_TILE):
                    if g == 0:
                        acc[(m, c)] = psum.tile([P, N_TILE], F32, tag="bank", name="acc%d_%d" % (m, c))
                    one_pass(acc[(m, c)], a_codes, a_scales, m, 0, g, c, 0)
        weight_step()
        sum_sq = const.tile([P, len(token_tiles)], F32)
        for m, (b, i) in enumerate(token_tiles):
            for c in range(0, D, N_TILE):
                nc.vector.tensor_tensor(
                    out=x1[m][:, c : c + N_TILE], in0=acc[(m, c)][:], in1=x1[m][:, c : c + N_TILE], op=ALU.add
                )
            nc.sync.dma_start(out=x1_rows[b, i], in_=x1[m][:])
            squares = work.tile([P, D], BF16)
            nc.scalar.activation(
                out=squares[:], in_=x1[m][:], func=ACT.Square, accum_out=sum_sq[:, m : m + 1]
            )

        rms = const.tile([P, len(token_tiles)], F32)
        nc.scalar.activation(out=rms[:], in_=sum_sq[:], func=ACT.Sqrt, scale=1.0 / D, bias=eps[:])
        weight_step()
        inv_rms = const.tile([P, len(token_tiles)], F32)
        nc.vector.reciprocal(out=inv_rms[:], in_=rms[:])
        n_codes = acts.tile([P, len(token_tiles), PASSES, P], U32, align_bytes=64)
        n_scales = acts.tile([P, len(token_tiles), PASSES, P], U8, align_bytes=64)
        g2_all = spread(g2_row, "g2_all")
        for m in range(len(token_tiles)):
            n_sb = work.tile([P, D], BF16)
            for c in range(0, D, N_TILE):
                nc.vector.scalar_tensor_tensor(
                    out=n_sb[:, c : c + N_TILE],
                    in0=x1[m][:, c : c + N_TILE],
                    scalar=inv_rms[:, m : m + 1],
                    in1=g2_all[c][:],
                    op0=ALU.mult,
                    op1=ALU.mult,
                )
            grouped_n = transpose_and_group(lambda c: n_sb[:, c * P : (c + 1) * P])
            weight_step()
            quantise_tokens(grouped_n, n_codes[:, m], n_scales[:, m])
        weight_step()

        for q in range(1, len(groups)):
            c0, width = groups[q][0][1], groups[q][0][2]
            cols = piece_cols[q]
            for c in range(0, width, cols):
                for m, (b, i) in enumerate(token_tiles):
                    u = psum.tile([P, cols], F32, tag="bank")
                    v = psum.tile([P, cols], F32, tag="bank")
                    for j, bank in enumerate((u, v)):
                        for g in range(PASSES):
                            one_pass(bank, n_codes, n_scales, m, q, g, c, j)
                    gate = out_pool.tile([P, cols], F32)
                    nc.scalar.activation(out=gate[:], in_=u[:], func=ACT.Silu)
                    weight_step()
                    h_sb = out_pool.tile([P, cols], F32, bufs=H_BUFS)
                    nc.vector.tensor_tensor(out=h_sb[:], in0=v[:], in1=gate[:], op=ALU.mult)
                    nc.sync.dma_start(out=h_rows[b, i][:, c0 + c : c0 + c + cols], in_=h_sb[:])
